import numpy as np
import ml_dtypes

BF16 = ml_dtypes.bfloat16


def bf(x):
    return np.asarray(x, np.float32).astype(BF16)


def f32(x):
    return np.asarray(x, np.float32)


def f64(x):
    return np.asarray(x).astype(np.float64)


def striped(idx):
    return np.tile(idx.reshape(-1, 16).T, (8, 1))


C, S, N = 256, 1024, 128


def setup_inputs():
    x = bf(4.0 * np.random.standard_normal((N, C)))
    adj = bf(np.random.uniform(size=(N, N)) * np.random.uniform(0.25, 1.75, size=(N, 1)))
    w1 = bf(2.0 * np.random.standard_normal((C, C)) / np.sqrt(C))
    b1 = f32(0.1 * np.random.standard_normal((C, 1)))
    base = f32(np.random.standard_normal((C, S)))
    return {"x": x, "adj": adj, "w1": w1, "b1": b1, "base": base, "offs": striped(np.random.permutation(S)[:N])}


def reference(x, adj, w1, b1, base, offs):
    idx = offs[:16].T.reshape(-1)
    a = f64(adj)
    d = 1.0 / np.sqrt(a.sum(axis=1))
    adjn = d[:, None] * a * d[None, :]
    agg = adjn @ f64(x)
    z = f64(w1).T @ agg.T + f64(b1)
    out = f64(base).copy()
    out[:, idx] = z
    return out

@@ -1,0 +1,82 @@
+import concourse.mybir as mybir
+from concourse.masks import make_identity
+
+P = 128
+C = 256
+S = 1024
+BLOCKS = C // P
+
+FLOPS = 2 * P * P * C + 2 * P * C * C
+
+BF16, F32, U16 = mybir.dt.bfloat16, mybir.dt.float32, mybir.dt.uint16
+MULT, ADD = mybir.AluOpType.mult, mybir.AluOpType.add
+RSQRT = mybir.ActivationFunctionType.Abs_reciprocal_sqrt
+
+
+def tile_multilayergnn_kernel(tc, x, adj, w1, b1, base, offs, out):
+    nc = tc.nc
+    with (
+        tc.tile_pool(name="held", bufs=1) as held,
+        tc.psum_pool(name="psum", bufs=1) as psum,
+    ):
+        adj_sb = held.tile([P, P], BF16, name="adj_sb")
+        nc.sync.dma_start(adj_sb[:], adj)
+        x_sb = held.tile([P, C], BF16, name="x_sb")
+        nc.sync.dma_start(x_sb[:], x)
+        offsets = held.tile([P, P // 16], U16, name="offsets")
+        nc.sync.dma_start(offsets[:], offs)
+        w1_sb = held.tile([P, BLOCKS, C], BF16, name="w1_sb")
+        nc.sync.dma_start(w1_sb[:], w1.rearrange("(kb p) c -> p kb c", p=P))
+        biases = [held.tile([P, 1], F32, name=f"bias{cb}") for cb in range(BLOCKS)]
+        for cb in range(BLOCKS):
+            nc.sync.dma_start(biases[cb][:], b1[cb * P : (cb + 1) * P, :])
+        windows = [held.tile([P, S], F32, name=f"window{cb}") for cb in range(BLOCKS)]
+        nc.sync.dma_start(windows[0][:], base[0:P, :])
+        nc.scalar.dma_start(windows[1][:], base[P : 2 * P, :])
+
+        identity = held.tile([P, P], BF16, name="identity")
+        make_identity(nc, identity[:])
+        ones = held.tile([P, P], BF16, name="ones")
+        nc.gpsimd.memset(ones[:], 1.0)
+        bias_rows = [held.tile([P, P], F32, name=f"bias_rows{cb}") for cb in range(BLOCKS)]
+        for cb in range(BLOCKS):
+            nc.gpsimd.tensor_copy(bias_rows[cb][:], biases[cb][:].to_broadcast([P, P]))
+
+        deg = held.tile([P, 1], F32, name="deg")
+        nc.vector.reduce_sum(deg[:], adj_sb[:], axis=mybir.AxisListType.X)
+        d = held.tile([P, 1], F32, name="d")
+        nc.scalar.activation(d[:], deg[:], RSQRT)
+
+        adjT_ps = psum.tile([P, P], BF16, name="adjT_ps")
+        nc.tensor.transpose(adjT_ps[:], adj_sb[:], identity[:])
+        adjT = held.tile([P, P], BF16, name="adjT")
+        nc.vector.tensor_copy(adjT[:], adjT_ps[:])
+
+        xs = held.tile([P, C], BF16, name="xs")
+        nc.vector.tensor_scalar(xs[:], x_sb[:], d[:], None, op0=MULT)
+
+        deg_row_ps = psum.tile([P, P], F32, name="deg_row_ps")
+        nc.tensor.matmul(deg_row_ps[:], ones[:], adjT[:], start=True, stop=True)
+        d_row = held.tile([P, P], F32, name="d_row")
+        nc.scalar.activation(d_row[:], deg_row_ps[:], RSQRT)
+
+        aggT = held.tile([P, BLOCKS, P], BF16, name="aggT")
+        for kb in range(BLOCKS):
+            agg_ps = psum.tile([P, P], F32, name=f"agg_ps{kb}")
+            nc.tensor.matmul(agg_ps[:], xs[:, kb * P : (kb + 1) * P], adjT[:], start=True, stop=True)
+            nc.vector.tensor_tensor(aggT[:, kb, :], agg_ps[:], d_row[:], MULT)
+
+        for cb in range(BLOCKS):
+            z_ps = psum.tile([P, P], F32, name=f"z_ps{cb}")
+            for kb in range(BLOCKS):
+                nc.tensor.matmul(
+                    z_ps[:],
+                    w1_sb[:, kb, cb * P : (cb + 1) * P],
+                    aggT[:, kb, :],
+                    start=(kb == 0),
+                    stop=(kb == BLOCKS - 1),
+                )
+            z_sb = held.tile([P, P], F32, name=f"z_sb{cb}")
+            nc.scalar.copy(z_sb[:], z_ps[:])
+            nc.vector.tensor_tensor(windows[cb][:].indirect(offsets[:]), z_sb[:], bias_rows[cb][:], ADD)
+            nc.sync.dma_start(out[cb * P : (cb + 1) * P, :], windows[cb][:])

@@ -34,6 +34,10 @@ def tile_multilayergnn_kernel(tc, x, adj, w1, b1, base, offs, out):
         nc.sync.dma_start(windows[0][:], base[0:P, :])
         nc.scalar.dma_start(windows[1][:], base[P : 2 * P, :])
 
+        scratch = held.tile([P, 1], F32, name="scratch")
+        nc.vector.memset(scratch[:], 1.0)
+        nc.scalar.activation(scratch[:], scratch[:], RSQRT)
+
         identity = held.tile([P, P], BF16, name="identity")
         make_identity(nc, identity[:])
         ones = held.tile([P, P], BF16, name="ones")

@@ -23,20 +23,16 @@ def tile_multilayergnn_kernel(tc, x, adj, w1, b1, base, offs, out):
         nc.sync.dma_start(adj_sb[:], adj)
         x_sb = held.tile([P, C], BF16, name="x_sb")
         nc.sync.dma_start(x_sb[:], x)
-        offsets = held.tile([P, P // 16], U16, name="offsets")
-        nc.sync.dma_start(offsets[:], offs)
         w1_sb = held.tile([P, BLOCKS, C], BF16, name="w1_sb")
         nc.sync.dma_start(w1_sb[:], w1.rearrange("(kb p) c -> p kb c", p=P))
+        offsets = held.tile([P, P // 16], U16, name="offsets")
+        nc.sync.dma_start(offsets[:], offs)
         biases = [held.tile([P, 1], F32, name=f"bias{cb}") for cb in range(BLOCKS)]
         for cb in range(BLOCKS):
             nc.sync.dma_start(biases[cb][:], b1[cb * P : (cb + 1) * P, :])
         windows = [held.tile([P, S], F32, name=f"window{cb}") for cb in range(BLOCKS)]
-        nc.sync.dma_start(windows[0][:], base[0:P, :])
-        nc.scalar.dma_start(windows[1][:], base[P : 2 * P, :])
-
-        scratch = held.tile([P, 1], F32, name="scratch")
-        nc.vector.memset(scratch[:], 1.0)
-        nc.scalar.activation(scratch[:], scratch[:], RSQRT)
+        for cb in range(BLOCKS):
+            nc.sync.dma_start(windows[cb][:], base[cb * P : (cb + 1) * P, :])
 
         identity = held.tile([P, P], BF16, name="identity")
         make_identity(nc, identity[:])

@@ -5,6 +5,8 @@ P = 128
 C = 256
 S = 1024
 BLOCKS = C // P
+BANK = 512
+WARM_UP = 4
 
 FLOPS = 2 * P * P * C + 2 * P * C * C
 
@@ -33,6 +35,12 @@ def tile_multilayergnn_kernel(tc, x, adj, w1, b1, base, offs, out):
         windows = [held.tile([P, S], F32, name=f"window{cb}") for cb in range(BLOCKS)]
         for cb in range(BLOCKS):
             nc.sync.dma_start(windows[cb][:], base[cb * P : (cb + 1) * P, :])
+
+        filler = held.tile([P, BANK], BF16, name="filler")
+        nc.vector.memset(filler[:], 0.0)
+        filler_ps = psum.tile([P, BANK], F32, name="filler_ps")
+        for i in range(WARM_UP):
+            nc.tensor.matmul(filler_ps[:], filler[:, 0:P], filler[:], start=True, stop=True)
 
         identity = held.tile([P, P], BF16, name="identity")
         make_identity(nc, identity[:])

@@ -5,8 +5,6 @@ P = 128
 C = 256
 S = 1024
 BLOCKS = C // P
-BANK = 512
-WARM_UP = 4
 
 FLOPS = 2 * P * P * C + 2 * P * C * C
 
@@ -35,12 +33,6 @@ def tile_multilayergnn_kernel(tc, x, adj, w1, b1, base, offs, out):
         windows = [held.tile([P, S], F32, name=f"window{cb}") for cb in range(BLOCKS)]
         for cb in range(BLOCKS):
             nc.sync.dma_start(windows[cb][:], base[cb * P : (cb + 1) * P, :])
-
-        filler = held.tile([P, BANK], BF16, name="filler")
-        nc.vector.memset(filler[:], 0.0)
-        filler_ps = psum.tile([P, BANK], F32, name="filler_ps")
-        for i in range(WARM_UP):
-            nc.tensor.matmul(filler_ps[:], filler[:, 0:P], filler[:], start=True, stop=True)
 
         identity = held.tile([P, P], BF16, name="identity")
         make_identity(nc, identity[:])
@@ -85,6 +77,6 @@ def tile_multilayergnn_kernel(tc, x, adj, w1, b1, base, offs, out):
                     stop=(kb == BLOCKS - 1),
                 )
             z_sb = held.tile([P, P], F32, name=f"z_sb{cb}")
-            nc.scalar.copy(z_sb[:], z_ps[:])
+            nc.vector.tensor_copy(z_sb[:], z_ps[:])
             nc.vector.tensor_tensor(windows[cb][:].indirect(offsets[:]), z_sb[:], bias_rows[cb][:], ADD)
             nc.sync.dma_start(out[cb * P : (cb + 1) * P, :], windows[cb][:])

@@ -38,9 +38,6 @@ def tile_multilayergnn_kernel(tc, x, adj, w1, b1, base, offs, out):
         make_identity(nc, identity[:])
         ones = held.tile([P, P], BF16, name="ones")
         nc.gpsimd.memset(ones[:], 1.0)
-        bias_rows = [held.tile([P, P], F32, name=f"bias_rows{cb}") for cb in range(BLOCKS)]
-        for cb in range(BLOCKS):
-            nc.gpsimd.tensor_copy(bias_rows[cb][:], biases[cb][:].to_broadcast([P, P]))
 
         deg = held.tile([P, 1], F32, name="deg")
         nc.vector.reduce_sum(deg[:], adj_sb[:], axis=mybir.AxisListType.X)
@@ -60,6 +57,10 @@ def tile_multilayergnn_kernel(tc, x, adj, w1, b1, base, offs, out):
         d_row = held.tile([P, P], F32, name="d_row")
         nc.scalar.activation(d_row[:], deg_row_ps[:], RSQRT)
 
+        bias_rows = [held.tile([P, P], F32, name=f"bias_rows{cb}") for cb in range(BLOCKS)]
+        for cb in range(BLOCKS):
+            nc.scalar.copy(bias_rows[cb][:], biases[cb][:].to_broadcast([P, P]))
+
         aggT = held.tile([P, BLOCKS, P], BF16, name="aggT")
         for kb in range(BLOCKS):
             agg_ps = psum.tile([P, P], F32, name=f"agg_ps{kb}")
@@ -77,6 +78,6 @@ def tile_multilayergnn_kernel(tc, x, adj, w1, b1, base, offs, out):
                     stop=(kb == BLOCKS - 1),
                 )
             z_sb = held.tile([P, P], F32, name=f"z_sb{cb}")
-            nc.vector.tensor_copy(z_sb[:], z_ps[:])
+            nc.scalar.copy(z_sb[:], z_ps[:])
             nc.vector.tensor_tensor(windows[cb][:].indirect(offsets[:]), z_sb[:], bias_rows[cb][:], ADD)
             nc.sync.dma_start(out[cb * P : (cb + 1) * P, :], windows[cb][:])

@@ -49,8 +49,8 @@ def tile_multilayergnn_kernel(tc, x, adj, w1, b1, base, offs, out):
         adjT = held.tile([P, P], BF16, name="adjT")
         nc.vector.tensor_copy(adjT[:], adjT_ps[:])
 
-        xs = held.tile([P, C], BF16, name="xs")
-        nc.vector.tensor_scalar(xs[:], x_sb[:], d[:], None, op0=MULT)
+        adjT_scaled = held.tile([P, P], BF16, name="adjT_scaled")
+        nc.vector.tensor_scalar(adjT_scaled[:], adjT[:], d[:], None, op0=MULT)
 
         deg_row_ps = psum.tile([P, P], F32, name="deg_row_ps")
         nc.tensor.matmul(deg_row_ps[:], ones[:], adjT[:], start=True, stop=True)
@@ -64,7 +64,7 @@ def tile_multilayergnn_kernel(tc, x, adj, w1, b1, base, offs, out):
         aggT = held.tile([P, BLOCKS, P], BF16, name="aggT")
         for kb in range(BLOCKS):
             agg_ps = psum.tile([P, P], F32, name=f"agg_ps{kb}")
-            nc.tensor.matmul(agg_ps[:], xs[:, kb * P : (kb + 1) * P], adjT[:], start=True, stop=True)
+            nc.tensor.matmul(agg_ps[:], x_sb[:, kb * P : (kb + 1) * P], adjT_scaled[:], start=True, stop=True)
             nc.vector.tensor_tensor(aggT[:, kb, :], agg_ps[:], d_row[:], MULT)
 
         for cb in range(BLOCKS):

@@ -36,8 +36,8 @@ def tile_multilayergnn_kernel(tc, x, adj, w1, b1, base, offs, out):
 
         identity = held.tile([P, P], BF16, name="identity")
         make_identity(nc, identity[:])
-        ones = held.tile([P, P], BF16, name="ones")
-        nc.gpsimd.memset(ones[:], 1.0)
+        identity_f32 = held.tile([P, P], F32, name="identity_f32")
+        make_identity(nc, identity_f32[:])
 
         deg = held.tile([P, 1], F32, name="deg")
         nc.vector.reduce_sum(deg[:], adj_sb[:], axis=mybir.AxisListType.X)
@@ -46,14 +46,12 @@ def tile_multilayergnn_kernel(tc, x, adj, w1, b1, base, offs, out):
 
         adjT_ps = psum.tile([P, P], BF16, name="adjT_ps")
         nc.tensor.transpose(adjT_ps[:], adj_sb[:], identity[:])
-        adjT = held.tile([P, P], BF16, name="adjT")
-        nc.vector.tensor_copy(adjT[:], adjT_ps[:])
 
         adjT_scaled = held.tile([P, P], BF16, name="adjT_scaled")
-        nc.vector.tensor_scalar(adjT_scaled[:], adjT[:], d[:], None, op0=MULT)
+        nc.vector.tensor_scalar(adjT_scaled[:], adjT_ps[:], d[:], None, op0=MULT)
 
         deg_row_ps = psum.tile([P, P], F32, name="deg_row_ps")
-        nc.tensor.matmul(deg_row_ps[:], ones[:], adjT[:], start=True, stop=True)
+        nc.tensor.transpose(deg_row_ps[:], deg[:].to_broadcast([P, P]), identity_f32[:])
         d_row = held.tile([P, P], F32, name="d_row")
         nc.scalar.activation(d_row[:], deg_row_ps[:], RSQRT)
 
@@ -78,6 +76,9 @@ def tile_multilayergnn_kernel(tc, x, adj, w1, b1, base, offs, out):
                     stop=(kb == BLOCKS - 1),
                 )
             z_sb = held.tile([P, P], F32, name=f"z_sb{cb}")
-            nc.scalar.copy(z_sb[:], z_ps[:])
+            if cb == 0:
+                nc.vector.tensor_copy(z_sb[:], z_ps[:])
+            else:
+                nc.scalar.copy(z_sb[:], z_ps[:])
             nc.vector.tensor_tensor(windows[cb][:].indirect(offsets[:]), z_sb[:], bias_rows[cb][:], ADD)
             nc.sync.dma_start(out[cb * P : (cb + 1) * P, :], windows[cb][:])

@@ -5,6 +5,7 @@ P = 128
 C = 256
 S = 1024
 BLOCKS = C // P
+HALVES = (slice(0, P // 2), slice(P // 2, P))
 
 FLOPS = 2 * P * P * C + 2 * P * C * C
 
@@ -18,6 +19,8 @@ def tile_multilayergnn_kernel(tc, x, adj, w1, b1, base, offs, out):
     with (
         tc.tile_pool(name="held", bufs=1) as held,
         tc.psum_pool(name="psum", bufs=1) as psum,
+        tc.psum_pool(name="psum_agg", bufs=BLOCKS * len(HALVES)) as psum_agg,
+        tc.psum_pool(name="psum_z", bufs=2) as psum_z,
     ):
         adj_sb = held.tile([P, P], BF16, name="adj_sb")
         nc.sync.dma_start(adj_sb[:], adj)
@@ -48,37 +51,41 @@ def tile_multilayergnn_kernel(tc, x, adj, w1, b1, base, offs, out):
         nc.tensor.transpose(adjT_ps[:], adj_sb[:], identity[:])
 
         adjT_scaled = held.tile([P, P], BF16, name="adjT_scaled")
-        nc.vector.tensor_scalar(adjT_scaled[:], adjT_ps[:], d[:], None, op0=MULT)
+        for half in HALVES:
+            nc.vector.tensor_scalar(adjT_scaled[:, half], adjT_ps[:, half], d[:], None, op0=MULT)
 
         deg_row_ps = psum.tile([P, P], F32, name="deg_row_ps")
         nc.tensor.transpose(deg_row_ps[:], deg[:].to_broadcast([P, P]), identity_f32[:])
         d_row = held.tile([P, P], F32, name="d_row")
-        nc.scalar.activation(d_row[:], deg_row_ps[:], RSQRT)
+        for half in HALVES:
+            nc.scalar.activation(d_row[:, half], deg_row_ps[:, half], RSQRT)
 
         bias_rows = [held.tile([P, P], F32, name=f"bias_rows{cb}") for cb in range(BLOCKS)]
         for cb in range(BLOCKS):
             nc.scalar.copy(bias_rows[cb][:], biases[cb][:].to_broadcast([P, P]))
 
         aggT = held.tile([P, BLOCKS, P], BF16, name="aggT")
-        for kb in range(BLOCKS):
-            agg_ps = psum.tile([P, P], F32, name=f"agg_ps{kb}")
-            nc.tensor.matmul(agg_ps[:], x_sb[:, kb * P : (kb + 1) * P], adjT_scaled[:], start=True, stop=True)
-            nc.vector.tensor_tensor(aggT[:, kb, :], agg_ps[:], d_row[:], MULT)
+        for half in HALVES:
+            for kb in range(BLOCKS):
+                agg_ps = psum_agg.tile([P, P // 2], F32, name="agg_ps")
+                nc.tensor.matmul(agg_ps[:], x_sb[:, kb * P : (kb + 1) * P], adjT_scaled[:, half], start=True, stop=True)
+                nc.vector.tensor_tensor(aggT[:, kb, half], agg_ps[:], d_row[:, half], MULT)
 
         for cb in range(BLOCKS):
-            z_ps = psum.tile([P, P], F32, name=f"z_ps{cb}")
-            for kb in range(BLOCKS):
-                nc.tensor.matmul(
-                    z_ps[:],
-                    w1_sb[:, kb, cb * P : (cb + 1) * P],
-                    aggT[:, kb, :],
-                    start=(kb == 0),
-                    stop=(kb == BLOCKS - 1),
-                )
             z_sb = held.tile([P, P], F32, name=f"z_sb{cb}")
-            if cb == 0:
-                nc.vector.tensor_copy(z_sb[:], z_ps[:])
-            else:
-                nc.scalar.copy(z_sb[:], z_ps[:])
+            for half in HALVES:
+                z_ps = psum_z.tile([P, P // 2], F32, name="z_ps")
+                for kb in range(BLOCKS):
+                    nc.tensor.matmul(
+                        z_ps[:],
+                        w1_sb[:, kb, cb * P : (cb + 1) * P],
+                        aggT[:, kb, half],
+                        start=(kb == 0),
+                        stop=(kb == BLOCKS - 1),
+                    )
+                if cb == 0:
+                    nc.vector.tensor_copy(z_sb[:, half], z_ps[:])
+                else:
+                    nc.scalar.copy(z_sb[:, half], z_ps[:])
             nc.vector.tensor_tensor(windows[cb][:].indirect(offsets[:]), z_sb[:], bias_rows[cb][:], ADD)
             nc.sync.dma_start(out[cb * P : (cb + 1) * P, :], windows[cb][:])

@@ -12,6 +12,7 @@ FLOPS = 2 * P * P * C + 2 * P * C * C
 BF16, F32, U16 = mybir.dt.bfloat16, mybir.dt.float32, mybir.dt.uint16
 MULT, ADD = mybir.AluOpType.mult, mybir.AluOpType.add
 RSQRT = mybir.ActivationFunctionType.Abs_reciprocal_sqrt
+IDENTITY = mybir.ActivationFunctionType.Identity
 
 
 def tile_multilayergnn_kernel(tc, x, adj, w1, b1, base, offs, out):
@@ -37,10 +38,9 @@ def tile_multilayergnn_kernel(tc, x, adj, w1, b1, base, offs, out):
         for cb in range(BLOCKS):
             nc.sync.dma_start(windows[cb][:], base[cb * P : (cb + 1) * P, :])
 
-        identity = held.tile([P, P], BF16, name="identity")
-        make_identity(nc, identity[:])
         identity_f32 = held.tile([P, P], F32, name="identity_f32")
         make_identity(nc, identity_f32[:])
+        identity = identity_f32[:].bitcast(BF16)[:, 1::2]
 
         deg = held.tile([P, 1], F32, name="deg")
         nc.vector.reduce_sum(deg[:], adj_sb[:], axis=mybir.AxisListType.X)
@@ -48,7 +48,7 @@ def tile_multilayergnn_kernel(tc, x, adj, w1, b1, base, offs, out):
         nc.scalar.activation(d[:], deg[:], RSQRT)
 
         adjT_ps = psum.tile([P, P], BF16, name="adjT_ps")
-        nc.tensor.transpose(adjT_ps[:], adj_sb[:], identity[:])
+        nc.tensor.transpose(adjT_ps[:], adj_sb[:], identity)
 
         adjT_scaled = held.tile([P, P], BF16, name="adjT_scaled")
         for half in HALVES:
@@ -62,7 +62,7 @@ def tile_multilayergnn_kernel(tc, x, adj, w1, b1, base, offs, out):
 
         bias_rows = [held.tile([P, P], F32, name=f"bias_rows{cb}") for cb in range(BLOCKS)]
         for cb in range(BLOCKS):
-            nc.scalar.copy(bias_rows[cb][:], biases[cb][:].to_broadcast([P, P]))
+            nc.scalar.activation(bias_rows[cb][:], d_row[:], IDENTITY, bias=biases[cb][:], scale=0.0)
 
         aggT = held.tile([P, BLOCKS, P], BF16, name="aggT")
         for half in HALVES:
@@ -83,7 +83,7 @@ def tile_multilayergnn_kernel(tc, x, adj, w1, b1, base, offs, out):
                         start=(kb == 0),
                         stop=(kb == BLOCKS - 1),
                     )
-                if cb == 0:
+                if cb == 0 and half == HALVES[0]:
                     nc.vector.tensor_copy(z_sb[:, half], z_ps[:])
                 else:
                     nc.scalar.copy(z_sb[:, half], z_ps[:])

@@ -31,12 +31,13 @@ def tile_multilayergnn_kernel(tc, x, adj, w1, b1, base, offs, out):
         nc.sync.dma_start(w1_sb[:], w1.rearrange("(kb p) c -> p kb c", p=P))
         offsets = held.tile([P, P // 16], U16, name="offsets")
         nc.sync.dma_start(offsets[:], offs)
-        biases = [held.tile([P, 1], F32, name=f"bias{cb}") for cb in range(BLOCKS)]
-        for cb in range(BLOCKS):
-            nc.sync.dma_start(biases[cb][:], b1[cb * P : (cb + 1) * P, :])
+        biases = held.tile([P, BLOCKS], F32, name="biases")
+        nc.sync.dma_start(biases[:], b1.rearrange("(p cb) o -> p (cb o)", cb=BLOCKS))
+        base_blocks = base.rearrange("(p cb) s -> p cb s", cb=BLOCKS)
+        out_blocks = out.rearrange("(p cb) s -> p cb s", cb=BLOCKS)
         windows = [held.tile([P, S], F32, name=f"window{cb}") for cb in range(BLOCKS)]
         for cb in range(BLOCKS):
-            nc.sync.dma_start(windows[cb][:], base[cb * P : (cb + 1) * P, :])
+            nc.sync.dma_start(windows[cb][:], base_blocks[:, cb, :])
 
         identity_f32 = held.tile([P, P], F32, name="identity_f32")
         make_identity(nc, identity_f32[:])
@@ -62,7 +63,7 @@ def tile_multilayergnn_kernel(tc, x, adj, w1, b1, base, offs, out):
 
         bias_rows = [held.tile([P, P], F32, name=f"bias_rows{cb}") for cb in range(BLOCKS)]
         for cb in range(BLOCKS):
-            nc.scalar.activation(bias_rows[cb][:], d_row[:], IDENTITY, bias=biases[cb][:], scale=0.0)
+            nc.scalar.activation(bias_rows[cb][:], d_row[:], IDENTITY, bias=biases[:, cb : cb + 1], scale=0.0)
 
         aggT = held.tile([P, BLOCKS, P], BF16, name="aggT")
         for half in HALVES:
@@ -78,7 +79,7 @@ def tile_multilayergnn_kernel(tc, x, adj, w1, b1, base, offs, out):
                 for kb in range(BLOCKS):
                     nc.tensor.matmul(
                         z_ps[:],
-                        w1_sb[:, kb, cb * P : (cb + 1) * P],
+                        w1_sb[:, kb, cb::BLOCKS],
                         aggT[:, kb, half],
                         start=(kb == 0),
                         stop=(kb == BLOCKS - 1),
@@ -88,4 +89,4 @@ def tile_multilayergnn_kernel(tc, x, adj, w1, b1, base, offs, out):
                 else:
                     nc.scalar.copy(z_sb[:, half], z_ps[:])
             nc.vector.tensor_tensor(windows[cb][:].indirect(offsets[:]), z_sb[:], bias_rows[cb][:], ADD)
-            nc.sync.dma_start(out[cb * P : (cb + 1) * P, :], windows[cb][:])
+            nc.sync.dma_start(out_blocks[:, cb, :], windows[cb][:])

@@ -27,12 +27,12 @@ def tile_multilayergnn_kernel(tc, x, adj, w1, b1, base, offs, out):
         nc.sync.dma_start(adj_sb[:], adj)
         x_sb = held.tile([P, C], BF16, name="x_sb")
         nc.sync.dma_start(x_sb[:], x)
+        biases = held.tile([P, BLOCKS], F32, name="biases")
+        nc.sync.dma_start(biases[:], b1.rearrange("(p cb) o -> p (cb o)", cb=BLOCKS))
         w1_sb = held.tile([P, BLOCKS, C], BF16, name="w1_sb")
         nc.sync.dma_start(w1_sb[:], w1.rearrange("(kb p) c -> p kb c", p=P))
         offsets = held.tile([P, P // 16], U16, name="offsets")
         nc.sync.dma_start(offsets[:], offs)
-        biases = held.tile([P, BLOCKS], F32, name="biases")
-        nc.sync.dma_start(biases[:], b1.rearrange("(p cb) o -> p (cb o)", cb=BLOCKS))
         base_blocks = base.rearrange("(p cb) s -> p cb s", cb=BLOCKS)
         out_blocks = out.rearrange("(p cb) s -> p cb s", cb=BLOCKS)
         windows = [held.tile([P, S], F32, name=f"window{cb}") for cb in range(BLOCKS)]

@@ -58,8 +58,7 @@ def tile_multilayergnn_kernel(tc, x, adj, w1, b1, base, offs, out):
         deg_row_ps = psum.tile([P, P], F32, name="deg_row_ps")
         nc.tensor.transpose(deg_row_ps[:], deg[:].to_broadcast([P, P]), identity_f32[:])
         d_row = held.tile([P, P], F32, name="d_row")
-        for half in HALVES:
-            nc.scalar.activation(d_row[:, half], deg_row_ps[:, half], RSQRT)
+        nc.scalar.activation(d_row[:], deg_row_ps[:], RSQRT)
 
         bias_rows = [held.tile([P, P], F32, name=f"bias_rows{cb}") for cb in range(BLOCKS)]
         for cb in range(BLOCKS):
@@ -84,9 +83,6 @@ def tile_multilayergnn_kernel(tc, x, adj, w1, b1, base, offs, out):
                         start=(kb == 0),
                         stop=(kb == BLOCKS - 1),
                     )
-                if cb == 0 and half == HALVES[0]:
-                    nc.vector.tensor_copy(z_sb[:, half], z_ps[:])
-                else:
-                    nc.scalar.copy(z_sb[:, half], z_ps[:])
+                nc.scalar.copy(z_sb[:, half], z_ps[:])
             nc.vector.tensor_tensor(windows[cb][:].indirect(offsets[:]), z_sb[:], bias_rows[cb][:], ADD)
             nc.sync.dma_start(out_blocks[:, cb, :], windows[cb][:])

@@ -10,9 +10,9 @@ HALVES = (slice(0, P // 2), slice(P // 2, P))
 FLOPS = 2 * P * P * C + 2 * P * C * C
 
 BF16, F32, U16 = mybir.dt.bfloat16, mybir.dt.float32, mybir.dt.uint16
+IDENTITY = mybir.ActivationFunctionType.Identity
 MULT, ADD = mybir.AluOpType.mult, mybir.AluOpType.add
 RSQRT = mybir.ActivationFunctionType.Abs_reciprocal_sqrt
-IDENTITY = mybir.ActivationFunctionType.Identity
 
 
 def tile_multilayergnn_kernel(tc, x, adj, w1, b1, base, offs, out):
@@ -61,8 +61,8 @@ def tile_multilayergnn_kernel(tc, x, adj, w1, b1, base, offs, out):
         nc.scalar.activation(d_row[:], deg_row_ps[:], RSQRT)
 
         bias_rows = [held.tile([P, P], F32, name=f"bias_rows{cb}") for cb in range(BLOCKS)]
-        for cb in range(BLOCKS):
-            nc.scalar.activation(bias_rows[cb][:], d_row[:], IDENTITY, bias=biases[:, cb : cb + 1], scale=0.0)
+        nc.vector.tensor_scalar(bias_rows[0][:], d_row[:], 0.0, biases[:, 0:1], op0=MULT, op1=ADD)
+        nc.scalar.activation(bias_rows[1][:], d_row[:], IDENTITY, bias=biases[:, 1:2], scale=0.0)
 
         aggT = held.tile([P, BLOCKS, P], BF16, name="aggT")
         for half in HALVES:

import concourse.mybir as mybir
from concourse.masks import make_identity

P = 128
C = 256
S = 1024
BLOCKS = C // P
HALVES = (slice(0, P // 2), slice(P // 2, P))

FLOPS = 2 * P * P * C + 2 * P * C * C

BF16, F32, U16 = mybir.dt.bfloat16, mybir.dt.float32, mybir.dt.uint16
IDENTITY = mybir.ActivationFunctionType.Identity
MULT, ADD = mybir.AluOpType.mult, mybir.AluOpType.add
RSQRT = mybir.ActivationFunctionType.Abs_reciprocal_sqrt


def tile_multilayergnn_kernel(tc, x, adj, w1, b1, base, offs, out):
    nc = tc.nc
    with (
        tc.tile_pool(name="held", bufs=1) as held,
        tc.psum_pool(name="psum", bufs=1) as psum,
        tc.psum_pool(name="psum_agg", bufs=BLOCKS * len(HALVES)) as psum_agg,
        tc.psum_pool(name="psum_z", bufs=2) as psum_z,
    ):
        adj_sb = held.tile([P, P], BF16, name="adj_sb")
        nc.sync.dma_start(adj_sb[:], adj)
        x_sb = held.tile([P, C], BF16, name="x_sb")
        nc.sync.dma_start(x_sb[:], x)
        biases = held.tile([P, BLOCKS], F32, name="biases")
        nc.sync.dma_start(biases[:], b1.rearrange("(p cb) o -> p (cb o)", cb=BLOCKS))
        w1_sb = held.tile([P, BLOCKS, C], BF16, name="w1_sb")
        nc.sync.dma_start(w1_sb[:], w1.rearrange("(kb p) c -> p kb c", p=P))
        offsets = held.tile([P, P // 16], U16, name="offsets")
        nc.sync.dma_start(offsets[:], offs)
        base_blocks = base.rearrange("(p cb) s -> p cb s", cb=BLOCKS)
        out_blocks = out.rearrange("(p cb) s -> p cb s", cb=BLOCKS)
        windows = [held.tile([P, S], F32, name=f"window{cb}") for cb in range(BLOCKS)]
        for cb in range(BLOCKS):
            nc.sync.dma_start(windows[cb][:], base_blocks[:, cb, :])

        identity_f32 = held.tile([P, P], F32, name="identity_f32")
        make_identity(nc, identity_f32[:])
        identity = identity_f32[:].bitcast(BF16)[:, 1::2]

        deg = held.tile([P, 1], F32, name="deg")
        nc.vector.reduce_sum(deg[:], adj_sb[:], axis=mybir.AxisListType.X)
        d = held.tile([P, 1], F32, name="d")
        nc.scalar.activation(d[:], deg[:], RSQRT)

        adjT_ps = psum.tile([P, P], BF16, name="adjT_ps")
        nc.tensor.transpose(adjT_ps[:], adj_sb[:], identity)

        adjT_scaled = held.tile([P, P], BF16, name="adjT_scaled")
        for half in HALVES:
            nc.vector.tensor_scalar(adjT_scaled[:, half], adjT_ps[:, half], d[:], None, op0=MULT)

        deg_row_ps = psum.tile([P, P], F32, name="deg_row_ps")
        nc.tensor.transpose(deg_row_ps[:], deg[:].to_broadcast([P, P]), identity_f32[:])
        d_row = held.tile([P, P], F32, name="d_row")
        nc.scalar.activation(d_row[:], deg_row_ps[:], RSQRT)

        bias_rows = [held.tile([P, P], F32, name=f"bias_rows{cb}") for cb in range(BLOCKS)]
        nc.vector.tensor_scalar(bias_rows[0][:], d_row[:], 0.0, biases[:, 0:1], op0=MULT, op1=ADD)
        nc.scalar.activation(bias_rows[1][:], d_row[:], IDENTITY, bias=biases[:, 1:2], scale=0.0)

        aggT = held.tile([P, BLOCKS, P], BF16, name="aggT")
        for half in HALVES:
            for kb in range(BLOCKS):
                agg_ps = psum_agg.tile([P, P // 2], F32, name="agg_ps")
                nc.tensor.matmul(agg_ps[:], x_sb[:, kb * P : (kb + 1) * P], adjT_scaled[:, half], start=True, stop=True)
                nc.vector.tensor_tensor(aggT[:, kb, half], agg_ps[:], d_row[:, half], MULT)

        for cb in range(BLOCKS):
            z_sb = held.tile([P, P], F32, name=f"z_sb{cb}")
            for half in HALVES:
                z_ps = psum_z.tile([P, P // 2], F32, name="z_ps")
                for kb in range(BLOCKS):
                    nc.tensor.matmul(
                        z_ps[:],
                        w1_sb[:, kb, cb::BLOCKS],
                        aggT[:, kb, half],
                        start=(kb == 0),
                        stop=(kb == BLOCKS - 1),
                    )
                nc.scalar.copy(z_sb[:, half], z_ps[:])
            nc.vector.tensor_tensor(windows[cb][:].indirect(offsets[:]), z_sb[:], bias_rows[cb][:], ADD)
            nc.sync.dma_start(out_blocks[:, cb, :], windows[cb][:])
